import numpy as np
import ml_dtypes

BF16 = ml_dtypes.bfloat16


def bf(x):
    return np.asarray(x, np.float32).astype(BF16)


def f32(x):
    return np.asarray(x, np.float32)


def f64(x):
    return np.asarray(x).astype(np.float64)


def striped(idx):
    return np.tile(idx.reshape(-1, 16).T, (8, 1))


D, S, N = 128, 512, 1024


def setup_inputs():
    return {
        "table": bf(np.random.standard_normal((D, S))),
        "qpu": bf(np.random.standard_normal((D, N))),
        "wq": bf(np.random.standard_normal((D, D)) / np.sqrt(2.0 * D)),
        "wp": bf(np.random.standard_normal((D, D)) / np.sqrt(2.0 * D)),
        "b1": f32(0.1 * np.random.standard_normal((D, 1))),
        "w2": bf(np.random.standard_normal((D, D)) / np.sqrt(D)),
        "b2": f32(0.5 * np.random.standard_normal((D, 1))),
        "ctx": f32(0.15 * np.random.standard_normal((D, 1))),
        "offs": striped(np.random.permutation(np.tile(np.arange(S), 2))[:N]),
    }


def reference(table, qpu, wq, wp, b1, w2, b2, ctx, offs):
    idx = offs[:16].T.reshape(-1)
    pre = f64(wq).T @ f64(table)[:, idx] + f64(wp).T @ f64(qpu) + f64(b1)
    h = np.maximum(pre, 0.0)
    keys = f64(w2).T @ h + f64(b2)
    return (f64(ctx) * keys).sum(axis=0, keepdims=True)

@@ -1,0 +1,66 @@
+import concourse.mybir as mybir
+
+BF16, F32, U16 = mybir.dt.bfloat16, mybir.dt.float32, mybir.dt.uint16
+RELU = mybir.ActivationFunctionType.Relu
+ADD = mybir.AluOpType.add
+
+D = 128
+S = 512
+N = 1024
+PIECE = 512
+PIECES = N // PIECE
+
+FLOPS = 2 * D * D * N * 3 + 2 * D * N
+
+
+def tile_policynetwork_kernel(tc, table, qpu, wq, wp, b1, w2, b2, ctx, offs, out):
+    nc = tc.nc
+    with (
+        tc.tile_pool(name="held", bufs=1) as held,
+        tc.tile_pool(name="work", bufs=PIECES) as work,
+        tc.psum_pool(name="psum", bufs=PIECES) as psum,
+    ):
+        offsets = held.tile([D, N // 16], U16, name="offsets")
+        nc.sync.dma_start(offsets[:], offs)
+
+        table_sb = held.tile([D, S], BF16, name="table_sb")
+        nc.sync.dma_start(table_sb[:], table)
+        qpu_sb = held.tile([D, N], BF16, name="qpu_sb")
+        nc.sync.dma_start(qpu_sb[:], qpu)
+
+        wq_sb = held.tile([D, D], BF16, name="wq_sb")
+        nc.scalar.dma_start(wq_sb[:], wq)
+        wp_sb = held.tile([D, D], BF16, name="wp_sb")
+        nc.scalar.dma_start(wp_sb[:], wp)
+        w2_sb = held.tile([D, D], BF16, name="w2_sb")
+        nc.scalar.dma_start(w2_sb[:], w2)
+
+        b1_sb = held.tile([D, 1], F32, name="b1_sb")
+        nc.gpsimd.dma_start(b1_sb[:], b1)
+        b2_sb = held.tile([D, 1], F32, name="b2_sb")
+        nc.gpsimd.dma_start(b2_sb[:], b2)
+        ctx_sb = held.tile([D, 1], F32, name="ctx_sb")
+        nc.gpsimd.dma_start(ctx_sb[:], ctx)
+
+        logits_sb = held.tile([1, N], F32, name="logits_sb")
+
+        for i in range(PIECES):
+            actions = slice(i * PIECE, (i + 1) * PIECE)
+            entries = offsets[:, i * (PIECE // 16) : (i + 1) * (PIECE // 16)]
+
+            pre = psum.tile([D, PIECE], F32, name="pre")
+            nc.tensor.matmul(pre[:], wq_sb[:], table_sb[:].indirect(entries), start=True, stop=False)
+            nc.tensor.matmul(pre[:], wp_sb[:], qpu_sb[:, actions], start=False, stop=True)
+            h = work.tile([D, PIECE], BF16, name="h")
+            nc.scalar.activation(h[:], pre[:], RELU, bias=b1_sb[:])
+
+            keys_ps = psum.tile([D, PIECE], F32, name="keys_ps")
+            nc.tensor.matmul(keys_ps[:], w2_sb[:], h[:], start=True, stop=True)
+            keys = work.tile([D, PIECE], F32, name="keys")
+            nc.vector.tensor_scalar(keys[:], keys_ps[:], b2_sb[:], None, ADD)
+
+            logits_ps = psum.tile([1, PIECE], F32, name="logits_ps")
+            nc.tensor.matmul(logits_ps[:], ctx_sb[:], keys[:], start=True, stop=True)
+            nc.vector.tensor_copy(logits_sb[:, actions], logits_ps[:])
+
+        nc.sync.dma_start(out, logits_sb[:])

@@ -9,6 +9,7 @@ S = 512
 N = 1024
 PIECE = 512
 PIECES = N // PIECE
+RUN = 8
 
 FLOPS = 2 * D * D * N * 3 + 2 * D * N
 
@@ -42,7 +43,7 @@ def tile_policynetwork_kernel(tc, table, qpu, wq, wp, b1, w2, b2, ctx, offs, out
         ctx_sb = held.tile([D, 1], F32, name="ctx_sb")
         nc.gpsimd.dma_start(ctx_sb[:], ctx)
 
-        logits_sb = held.tile([1, N], F32, name="logits_sb")
+        keys = held.tile([D, N], F32, name="keys")
 
         for i in range(PIECES):
             actions = slice(i * PIECE, (i + 1) * PIECE)
@@ -56,11 +57,12 @@ def tile_policynetwork_kernel(tc, table, qpu, wq, wp, b1, w2, b2, ctx, offs, out
 
             keys_ps = psum.tile([D, PIECE], F32, name="keys_ps")
             nc.tensor.matmul(keys_ps[:], w2_sb[:], h[:], start=True, stop=True)
-            keys = work.tile([D, PIECE], F32, name="keys")
-            nc.vector.tensor_scalar(keys[:], keys_ps[:], b2_sb[:], None, ADD)
+            nc.vector.tensor_scalar(keys[:, actions], keys_ps[:], b2_sb[:], None, ADD)
 
-            logits_ps = psum.tile([1, PIECE], F32, name="logits_ps")
-            nc.tensor.matmul(logits_ps[:], ctx_sb[:], keys[:], start=True, stop=True)
-            nc.vector.tensor_copy(logits_sb[:, actions], logits_ps[:])
-
-        nc.sync.dma_start(out, logits_sb[:])
+        keys_by_c = keys[:].rearrange("r (p c) -> r c p", c=RUN)
+        logits_ps = psum.tile([N // RUN, RUN], F32, name="logits_ps")
+        for c in range(RUN):
+            nc.tensor.matmul(logits_ps[:, c : c + 1], keys_by_c[:, c, :], ctx_sb[:], start=True, stop=True)
+        logits_sb = held.tile([N // RUN, RUN], F32, name="logits_sb")
+        nc.vector.tensor_copy(logits_sb[:], logits_ps[:])
+        nc.sync.dma_start(out.rearrange("o (p c) -> (o p) c", c=RUN), logits_sb[:])

@@ -9,7 +9,6 @@ S = 512
 N = 1024
 PIECE = 512
 PIECES = N // PIECE
-RUN = 8
 
 FLOPS = 2 * D * D * N * 3 + 2 * D * N
 
@@ -22,28 +21,28 @@ def tile_policynetwork_kernel(tc, table, qpu, wq, wp, b1, w2, b2, ctx, offs, out
         tc.psum_pool(name="psum", bufs=PIECES) as psum,
     ):
         offsets = held.tile([D, N // 16], U16, name="offsets")
-        nc.sync.dma_start(offsets[:], offs)
-
         table_sb = held.tile([D, S], BF16, name="table_sb")
-        nc.sync.dma_start(table_sb[:], table)
         qpu_sb = held.tile([D, N], BF16, name="qpu_sb")
-        nc.sync.dma_start(qpu_sb[:], qpu)
-
         wq_sb = held.tile([D, D], BF16, name="wq_sb")
-        nc.scalar.dma_start(wq_sb[:], wq)
         wp_sb = held.tile([D, D], BF16, name="wp_sb")
-        nc.scalar.dma_start(wp_sb[:], wp)
         w2_sb = held.tile([D, D], BF16, name="w2_sb")
-        nc.scalar.dma_start(w2_sb[:], w2)
-
         b1_sb = held.tile([D, 1], F32, name="b1_sb")
-        nc.gpsimd.dma_start(b1_sb[:], b1)
         b2_sb = held.tile([D, 1], F32, name="b2_sb")
-        nc.gpsimd.dma_start(b2_sb[:], b2)
         ctx_sb = held.tile([D, 1], F32, name="ctx_sb")
-        nc.gpsimd.dma_start(ctx_sb[:], ctx)
 
-        keys = held.tile([D, N], F32, name="keys")
+        nc.sync.dma_start(offsets[:], offs)
+        nc.sync.dma_start(table_sb[:], table)
+        for i in range(PIECES):
+            actions = slice(i * PIECE, (i + 1) * PIECE)
+            nc.sync.dma_start(qpu_sb[:, actions], qpu[:, actions])
+        nc.scalar.dma_start(wq_sb[:], wq)
+        nc.scalar.dma_start(wp_sb[:], wp)
+        nc.scalar.dma_start(b1_sb[:], b1)
+        nc.scalar.dma_start(w2_sb[:], w2)
+        nc.scalar.dma_start(b2_sb[:], b2)
+        nc.scalar.dma_start(ctx_sb[:], ctx)
+
+        logits_sb = held.tile([1, N], F32, name="logits_sb")
 
         for i in range(PIECES):
             actions = slice(i * PIECE, (i + 1) * PIECE)
@@ -57,12 +56,11 @@ def tile_policynetwork_kernel(tc, table, qpu, wq, wp, b1, w2, b2, ctx, offs, out
 
             keys_ps = psum.tile([D, PIECE], F32, name="keys_ps")
             nc.tensor.matmul(keys_ps[:], w2_sb[:], h[:], start=True, stop=True)
-            nc.vector.tensor_scalar(keys[:, actions], keys_ps[:], b2_sb[:], None, ADD)
+            keys = work.tile([D, PIECE], F32, name="keys")
+            nc.vector.tensor_scalar(keys[:], keys_ps[:], b2_sb[:], None, ADD)
 
-        keys_by_c = keys[:].rearrange("r (p c) -> r c p", c=RUN)
-        logits_ps = psum.tile([N // RUN, RUN], F32, name="logits_ps")
-        for c in range(RUN):
-            nc.tensor.matmul(logits_ps[:, c : c + 1], keys_by_c[:, c, :], ctx_sb[:], start=True, stop=True)
-        logits_sb = held.tile([N // RUN, RUN], F32, name="logits_sb")
-        nc.vector.tensor_copy(logits_sb[:], logits_ps[:])
-        nc.sync.dma_start(out.rearrange("o (p c) -> (o p) c", c=RUN), logits_sb[:])
+            logits_ps = psum.tile([1, PIECE], F32, name="logits_ps")
+            nc.tensor.matmul(logits_ps[:], ctx_sb[:], keys[:], start=True, stop=True)
+            nc.vector.tensor_copy(logits_sb[:, actions], logits_ps[:])
+
+        nc.sync.dma_start(out, logits_sb[:])

@@ -9,6 +9,7 @@ S = 512
 N = 1024
 PIECE = 512
 PIECES = N // PIECE
+WARM = 6
 
 FLOPS = 2 * D * D * N * 3 + 2 * D * N
 
@@ -41,6 +42,12 @@ def tile_policynetwork_kernel(tc, table, qpu, wq, wp, b1, w2, b2, ctx, offs, out
         nc.scalar.dma_start(w2_sb[:], w2)
         nc.scalar.dma_start(b2_sb[:], b2)
         nc.scalar.dma_start(ctx_sb[:], ctx)
+
+        zeros = held.tile([D, PIECE], BF16, name="zeros")
+        nc.vector.memset(zeros[:], 0.0)
+        unread = psum.tile([D, PIECE], F32, name="unread")
+        for turn in range(WARM):
+            nc.tensor.matmul(unread[:], zeros[:, :D], zeros[:], start=True, stop=True)
 
         logits_sb = held.tile([1, N], F32, name="logits_sb")
 

@@ -1,15 +1,14 @@
 import concourse.mybir as mybir
 
 BF16, F32, U16 = mybir.dt.bfloat16, mybir.dt.float32, mybir.dt.uint16
-RELU = mybir.ActivationFunctionType.Relu
-ADD = mybir.AluOpType.add
+IDENTITY = mybir.ActivationFunctionType.Identity
+ADD, MAX = mybir.AluOpType.add, mybir.AluOpType.max
 
 D = 128
 S = 512
 N = 1024
-PIECE = 512
-PIECES = N // PIECE
-WARM = 6
+PIECES = 4
+PIECE = N // PIECES
 
 FLOPS = 2 * D * D * N * 3 + 2 * D * N
 
@@ -19,7 +18,8 @@ def tile_policynetwork_kernel(tc, table, qpu, wq, wp, b1, w2, b2, ctx, offs, out
     with (
         tc.tile_pool(name="held", bufs=1) as held,
         tc.tile_pool(name="work", bufs=PIECES) as work,
-        tc.psum_pool(name="psum", bufs=PIECES) as psum,
+        tc.psum_pool(name="layer1", bufs=PIECES) as layer1,
+        tc.psum_pool(name="later", bufs=2) as later,
     ):
         offsets = held.tile([D, N // 16], U16, name="offsets")
         table_sb = held.tile([D, S], BF16, name="table_sb")
@@ -30,12 +30,12 @@ def tile_policynetwork_kernel(tc, table, qpu, wq, wp, b1, w2, b2, ctx, offs, out
         b1_sb = held.tile([D, 1], F32, name="b1_sb")
         b2_sb = held.tile([D, 1], F32, name="b2_sb")
         ctx_sb = held.tile([D, 1], F32, name="ctx_sb")
+        logits_sb = held.tile([1, N], F32, name="logits_sb")
 
         nc.sync.dma_start(offsets[:], offs)
         nc.sync.dma_start(table_sb[:], table)
-        for i in range(PIECES):
-            actions = slice(i * PIECE, (i + 1) * PIECE)
-            nc.sync.dma_start(qpu_sb[:, actions], qpu[:, actions])
+        nc.sync.dma_start(qpu_sb[:, : N // 2], qpu[:, : N // 2])
+        nc.sync.dma_start(qpu_sb[:, N // 2 :], qpu[:, N // 2 :])
         nc.scalar.dma_start(wq_sb[:], wq)
         nc.scalar.dma_start(wp_sb[:], wp)
         nc.scalar.dma_start(b1_sb[:], b1)
@@ -43,31 +43,28 @@ def tile_policynetwork_kernel(tc, table, qpu, wq, wp, b1, w2, b2, ctx, offs, out
         nc.scalar.dma_start(b2_sb[:], b2)
         nc.scalar.dma_start(ctx_sb[:], ctx)
 
-        zeros = held.tile([D, PIECE], BF16, name="zeros")
-        nc.vector.memset(zeros[:], 0.0)
-        unread = psum.tile([D, PIECE], F32, name="unread")
-        for turn in range(WARM):
-            nc.tensor.matmul(unread[:], zeros[:, :D], zeros[:], start=True, stop=True)
-
-        logits_sb = held.tile([1, N], F32, name="logits_sb")
-
+        pre = []
         for i in range(PIECES):
-            actions = slice(i * PIECE, (i + 1) * PIECE)
+            pre.append(layer1.tile([D, PIECE], F32, name="pre"))
             entries = offsets[:, i * (PIECE // 16) : (i + 1) * (PIECE // 16)]
+            nc.tensor.matmul(pre[i][:], wq_sb[:], table_sb[:].indirect(entries), start=True, stop=False)
 
-            pre = psum.tile([D, PIECE], F32, name="pre")
-            nc.tensor.matmul(pre[:], wq_sb[:], table_sb[:].indirect(entries), start=True, stop=False)
-            nc.tensor.matmul(pre[:], wp_sb[:], qpu_sb[:, actions], start=False, stop=True)
-            h = work.tile([D, PIECE], BF16, name="h")
-            nc.scalar.activation(h[:], pre[:], RELU, bias=b1_sb[:])
+        h = []
+        for i in range(PIECES):
+            nc.tensor.matmul(pre[i][:], wp_sb[:], qpu_sb[:, i * PIECE : (i + 1) * PIECE], start=False, stop=True)
+            h.append(work.tile([D, PIECE], BF16, name="h"))
+            nc.vector.tensor_scalar(h[i][:], pre[i][:], b1_sb[:], 0.0, ADD, MAX)
 
-            keys_ps = psum.tile([D, PIECE], F32, name="keys_ps")
-            nc.tensor.matmul(keys_ps[:], w2_sb[:], h[:], start=True, stop=True)
-            keys = work.tile([D, PIECE], F32, name="keys")
-            nc.vector.tensor_scalar(keys[:], keys_ps[:], b2_sb[:], None, ADD)
-
-            logits_ps = psum.tile([1, PIECE], F32, name="logits_ps")
-            nc.tensor.matmul(logits_ps[:], ctx_sb[:], keys[:], start=True, stop=True)
-            nc.vector.tensor_copy(logits_sb[:, actions], logits_ps[:])
+        keys = []
+        for i in range(PIECES + 1):
+            if i < PIECES:
+                keys_ps = later.tile([D, PIECE], F32, name="keys_ps")
+                nc.tensor.matmul(keys_ps[:], w2_sb[:], h[i][:], start=True, stop=True)
+                keys.append(work.tile([D, PIECE], F32, name="keys"))
+                nc.scalar.activation(keys[i][:], keys_ps[:], IDENTITY, bias=b2_sb[:])
+            if i > 0:
+                logits_ps = later.tile([1, PIECE], F32, name="logits_ps")
+                nc.tensor.matmul(logits_ps[:], ctx_sb[:], keys[i - 1][:], start=True, stop=True)
+                nc.vector.tensor_copy(logits_sb[:, (i - 1) * PIECE : i * PIECE], logits_ps[:])
 
         nc.sync.dma_start(out, logits_sb[:])

@@ -9,6 +9,7 @@ S = 512
 N = 1024
 PIECES = 4
 PIECE = N // PIECES
+WARM = 3
 
 FLOPS = 2 * D * D * N * 3 + 2 * D * N
 
@@ -34,14 +35,21 @@ def tile_policynetwork_kernel(tc, table, qpu, wq, wp, b1, w2, b2, ctx, offs, out
 
         nc.sync.dma_start(offsets[:], offs)
         nc.sync.dma_start(table_sb[:], table)
-        nc.sync.dma_start(qpu_sb[:, : N // 2], qpu[:, : N // 2])
-        nc.sync.dma_start(qpu_sb[:, N // 2 :], qpu[:, N // 2 :])
+        nc.sync.dma_start(qpu_sb[:], qpu)
+        nc.sync.dma_start(w2_sb[:], w2)
+        nc.sync.dma_start(b2_sb[:], b2)
+        nc.sync.dma_start(ctx_sb[:], ctx)
         nc.scalar.dma_start(wq_sb[:], wq)
         nc.scalar.dma_start(wp_sb[:], wp)
         nc.scalar.dma_start(b1_sb[:], b1)
-        nc.scalar.dma_start(w2_sb[:], w2)
-        nc.scalar.dma_start(b2_sb[:], b2)
-        nc.scalar.dma_start(ctx_sb[:], ctx)
+
+        zeros = held.tile([D, D], BF16, name="zeros")
+        nc.vector.memset(zeros[:], 0.0)
+        primed = held.tile([D, 1], F32, name="primed")
+        nc.scalar.activation(primed[:], zeros[:, 0:1], IDENTITY)
+        unread = layer1.tile([D, S], F32, name="unread", tag="pre")
+        for turn in range(WARM):
+            nc.tensor.matmul(unread[:], zeros[:], zeros[:, 0:1].to_broadcast([D, S]), start=True, stop=True)
 
         pre = []
         for i in range(PIECES):

@@ -1,8 +1,10 @@
 import concourse.mybir as mybir
+from concourse.masks import make_identity
 
 BF16, F32, U16 = mybir.dt.bfloat16, mybir.dt.float32, mybir.dt.uint16
-IDENTITY = mybir.ActivationFunctionType.Identity
-ADD, MAX = mybir.AluOpType.add, mybir.AluOpType.max
+IDENTITY, RELU = mybir.ActivationFunctionType.Identity, mybir.ActivationFunctionType.Relu
+ADD, MAX, MULT = mybir.AluOpType.add, mybir.AluOpType.max, mybir.AluOpType.mult
+X = mybir.AxisListType.X
 
 D = 128
 S = 512
@@ -10,6 +12,7 @@ N = 1024
 PIECES = 4
 PIECE = N // PIECES
 WARM = 3
+RUN = 8
 
 FLOPS = 2 * D * D * N * 3 + 2 * D * N
 
@@ -20,7 +23,7 @@ def tile_policynetwork_kernel(tc, table, qpu, wq, wp, b1, w2, b2, ctx, offs, out
         tc.tile_pool(name="held", bufs=1) as held,
         tc.tile_pool(name="work", bufs=PIECES) as work,
         tc.psum_pool(name="layer1", bufs=PIECES) as layer1,
-        tc.psum_pool(name="later", bufs=2) as later,
+        tc.psum_pool(name="layer2", bufs=PIECES) as layer2,
     ):
         offsets = held.tile([D, N // 16], U16, name="offsets")
         table_sb = held.tile([D, S], BF16, name="table_sb")
@@ -31,17 +34,16 @@ def tile_policynetwork_kernel(tc, table, qpu, wq, wp, b1, w2, b2, ctx, offs, out
         b1_sb = held.tile([D, 1], F32, name="b1_sb")
         b2_sb = held.tile([D, 1], F32, name="b2_sb")
         ctx_sb = held.tile([D, 1], F32, name="ctx_sb")
-        logits_sb = held.tile([1, N], F32, name="logits_sb")
 
         nc.sync.dma_start(offsets[:], offs)
         nc.sync.dma_start(table_sb[:], table)
         nc.sync.dma_start(qpu_sb[:], qpu)
         nc.sync.dma_start(w2_sb[:], w2)
         nc.sync.dma_start(b2_sb[:], b2)
-        nc.sync.dma_start(ctx_sb[:], ctx)
         nc.scalar.dma_start(wq_sb[:], wq)
         nc.scalar.dma_start(wp_sb[:], wp)
         nc.scalar.dma_start(b1_sb[:], b1)
+        nc.scalar.dma_start(ctx_sb[:], ctx)
 
         zeros = held.tile([D, D], BF16, name="zeros")
         nc.vector.memset(zeros[:], 0.0)
@@ -50,6 +52,20 @@ def tile_policynetwork_kernel(tc, table, qpu, wq, wp, b1, w2, b2, ctx, offs, out
         unread = layer1.tile([D, S], F32, name="unread", tag="pre")
         for turn in range(WARM):
             nc.tensor.matmul(unread[:], zeros[:], zeros[:, 0:1].to_broadcast([D, S]), start=True, stop=True)
+        identity = held.tile([D, D], F32, name="identity")
+        make_identity(nc, identity[:])
+
+        def bias_relu(i, h_i, pre_i):
+            if i % 2 == 0:
+                nc.vector.tensor_scalar(h_i, pre_i, b1_sb[:], 0.0, ADD, MAX)
+            else:
+                nc.scalar.activation(h_i, pre_i, RELU, bias=b1_sb[:])
+
+        def weigh(i, weighted_i, keys_i):
+            if i % 2 == 0:
+                nc.vector.tensor_scalar(weighted_i, keys_i, ctx_sb[:], ctx_b2[:], MULT, ADD)
+            else:
+                nc.scalar.activation(weighted_i, keys_i, IDENTITY, bias=ctx_b2[:], scale=ctx_sb[:])
 
         pre = []
         for i in range(PIECES):
@@ -61,18 +77,24 @@ def tile_policynetwork_kernel(tc, table, qpu, wq, wp, b1, w2, b2, ctx, offs, out
         for i in range(PIECES):
             nc.tensor.matmul(pre[i][:], wp_sb[:], qpu_sb[:, i * PIECE : (i + 1) * PIECE], start=False, stop=True)
             h.append(work.tile([D, PIECE], BF16, name="h"))
-            nc.vector.tensor_scalar(h[i][:], pre[i][:], b1_sb[:], 0.0, ADD, MAX)
+            bias_relu(i, h[i][:], pre[i][:])
 
-        keys = []
-        for i in range(PIECES + 1):
-            if i < PIECES:
-                keys_ps = later.tile([D, PIECE], F32, name="keys_ps")
-                nc.tensor.matmul(keys_ps[:], w2_sb[:], h[i][:], start=True, stop=True)
-                keys.append(work.tile([D, PIECE], F32, name="keys"))
-                nc.scalar.activation(keys[i][:], keys_ps[:], IDENTITY, bias=b2_sb[:])
-            if i > 0:
-                logits_ps = later.tile([1, PIECE], F32, name="logits_ps")
-                nc.tensor.matmul(logits_ps[:], ctx_sb[:], keys[i - 1][:], start=True, stop=True)
-                nc.vector.tensor_copy(logits_sb[:, (i - 1) * PIECE : i * PIECE], logits_ps[:])
+        ctx_b2 = held.tile([D, 1], F32, name="ctx_b2")
+        nc.vector.tensor_tensor(ctx_b2[:], ctx_sb[:], b2_sb[:], MULT)
 
-        nc.sync.dma_start(out, logits_sb[:])
+        weighted = held.tile([D, N], F32, name="weighted")
+        for i in range(PIECES):
+            keys_ps = layer2.tile([D, PIECE], F32, name="keys_ps")
+            nc.tensor.matmul(keys_ps[:], w2_sb[:], h[i][:], start=True, stop=True)
+            weigh(i, weighted[:, i * PIECE : (i + 1) * PIECE], keys_ps[:])
+
+        by_c = weighted[:].rearrange("r (p c) -> r c p", c=RUN)
+        logits = held.tile([N // RUN, RUN], F32, name="logits")
+        per_bank = S // D
+        for k in range(RUN // per_bank):
+            flipped = layer1.tile([N // RUN, per_bank, D], F32, name="flipped", tag="pre")
+            for c in range(per_bank):
+                nc.tensor.transpose(flipped[:, c, :], by_c[:, k * per_bank + c, :], identity[:])
+            nc.vector.tensor_reduce(logits[:, k * per_bank : (k + 1) * per_bank], flipped[:], X, ADD)
+
+        nc.sync.dma_start(out.rearrange("o (p c) -> (o p) c", c=RUN), logits[:])

@@ -1,18 +1,16 @@
 import concourse.mybir as mybir
-from concourse.masks import make_identity
 
 BF16, F32, U16 = mybir.dt.bfloat16, mybir.dt.float32, mybir.dt.uint16
 IDENTITY, RELU = mybir.ActivationFunctionType.Identity, mybir.ActivationFunctionType.Relu
-ADD, MAX, MULT = mybir.AluOpType.add, mybir.AluOpType.max, mybir.AluOpType.mult
-X = mybir.AxisListType.X
+ADD, MAX = mybir.AluOpType.add, mybir.AluOpType.max
 
 D = 128
 S = 512
 N = 1024
 PIECES = 4
 PIECE = N // PIECES
+GROUP = 32
 WARM = 3
-RUN = 8
 
 FLOPS = 2 * D * D * N * 3 + 2 * D * N
 
@@ -52,8 +50,6 @@ def tile_policynetwork_kernel(tc, table, qpu, wq, wp, b1, w2, b2, ctx, offs, out
         unread = layer1.tile([D, S], F32, name="unread", tag="pre")
         for turn in range(WARM):
             nc.tensor.matmul(unread[:], zeros[:], zeros[:, 0:1].to_broadcast([D, S]), start=True, stop=True)
-        identity = held.tile([D, D], F32, name="identity")
-        make_identity(nc, identity[:])
 
         def bias_relu(i, h_i, pre_i):
             if i % 2 == 0:
@@ -61,11 +57,17 @@ def tile_policynetwork_kernel(tc, table, qpu, wq, wp, b1, w2, b2, ctx, offs, out
             else:
                 nc.scalar.activation(h_i, pre_i, RELU, bias=b1_sb[:])
 
-        def weigh(i, weighted_i, keys_i):
+        def add_b2(i, keys_i, keys_ps_i):
             if i % 2 == 0:
-                nc.vector.tensor_scalar(weighted_i, keys_i, ctx_sb[:], ctx_b2[:], MULT, ADD)
+                nc.vector.tensor_scalar_add(keys_i, keys_ps_i, b2_sb[:])
             else:
-                nc.scalar.activation(weighted_i, keys_i, IDENTITY, bias=ctx_b2[:], scale=ctx_sb[:])
+                nc.scalar.activation(keys_i, keys_ps_i, IDENTITY, bias=b2_sb[:])
+
+        def copy_out(i, logits_i, sums_i):
+            if i % 2 == 0:
+                nc.vector.tensor_copy(logits_i, sums_i)
+            else:
+                nc.scalar.activation(logits_i, sums_i, IDENTITY)
 
         pre = []
         for i in range(PIECES):
@@ -79,22 +81,18 @@ def tile_policynetwork_kernel(tc, table, qpu, wq, wp, b1, w2, b2, ctx, offs, out
             h.append(work.tile([D, PIECE], BF16, name="h"))
             bias_relu(i, h[i][:], pre[i][:])
 
-        ctx_b2 = held.tile([D, 1], F32, name="ctx_b2")
-        nc.vector.tensor_tensor(ctx_b2[:], ctx_sb[:], b2_sb[:], MULT)
-
-        weighted = held.tile([D, N], F32, name="weighted")
+        keys = []
         for i in range(PIECES):
             keys_ps = layer2.tile([D, PIECE], F32, name="keys_ps")
             nc.tensor.matmul(keys_ps[:], w2_sb[:], h[i][:], start=True, stop=True)
-            weigh(i, weighted[:, i * PIECE : (i + 1) * PIECE], keys_ps[:])
+            keys.append(work.tile([D, PIECE], F32, name="keys"))
+            add_b2(i, keys[i][:], keys_ps[:])
 
-        by_c = weighted[:].rearrange("r (p c) -> r c p", c=RUN)
-        logits = held.tile([N // RUN, RUN], F32, name="logits")
-        per_bank = S // D
-        for k in range(RUN // per_bank):
-            flipped = layer1.tile([N // RUN, per_bank, D], F32, name="flipped", tag="pre")
-            for c in range(per_bank):
-                nc.tensor.transpose(flipped[:, c, :], by_c[:, k * per_bank + c, :], identity[:])
-            nc.vector.tensor_reduce(logits[:, k * per_bank : (k + 1) * per_bank], flipped[:], X, ADD)
-
-        nc.sync.dma_start(out.rearrange("o (p c) -> (o p) c", c=RUN), logits[:])
+        logits = held.tile([D, PIECE], F32, name="logits")
+        for i in range(PIECES):
+            sums = layer1.tile([D, PIECE], F32, name="sums", tag="pre")
+            row = slice(i * GROUP, i * GROUP + 1)
+            nc.tensor.matmul(sums[row, :], ctx_sb[:], keys[i][:], start=True, stop=True)
+            copy_out(i, logits[row, :], sums[row, :])
+            queue = nc.sync if i % 2 == 0 else nc.scalar
+            queue.dma_start(out[:, i * PIECE : (i + 1) * PIECE], logits[row, :])

@@ -2,7 +2,7 @@ import concourse.mybir as mybir
 
 BF16, F32, U16 = mybir.dt.bfloat16, mybir.dt.float32, mybir.dt.uint16
 IDENTITY, RELU = mybir.ActivationFunctionType.Identity, mybir.ActivationFunctionType.Relu
-ADD, MAX = mybir.AluOpType.add, mybir.AluOpType.max
+ADD, MAX, MULT = mybir.AluOpType.add, mybir.AluOpType.max, mybir.AluOpType.mult
 
 D = 128
 S = 512
@@ -10,9 +10,11 @@ N = 1024
 PIECES = 4
 PIECE = N // PIECES
 GROUP = 32
+GROUPS = D // GROUP
+SHARE = PIECE // GROUPS
 WARM = 3
 
-FLOPS = 2 * D * D * N * 3 + 2 * D * N
+FLOPS = 2 * D * D * N * 2 + 2 * D * D + 2 * D + 2 * D * N
 
 
 def tile_policynetwork_kernel(tc, table, qpu, wq, wp, b1, w2, b2, ctx, offs, out):
@@ -21,7 +23,8 @@ def tile_policynetwork_kernel(tc, table, qpu, wq, wp, b1, w2, b2, ctx, offs, out
         tc.tile_pool(name="held", bufs=1) as held,
         tc.tile_pool(name="work", bufs=PIECES) as work,
         tc.psum_pool(name="layer1", bufs=PIECES) as layer1,
-        tc.psum_pool(name="layer2", bufs=PIECES) as layer2,
+        tc.psum_pool(name="folded", bufs=1) as folded,
+        tc.psum_pool(name="summed", bufs=3) as summed,
     ):
         offsets = held.tile([D, N // 16], U16, name="offsets")
         table_sb = held.tile([D, S], BF16, name="table_sb")
@@ -30,26 +33,35 @@ def tile_policynetwork_kernel(tc, table, qpu, wq, wp, b1, w2, b2, ctx, offs, out
         wp_sb = held.tile([D, D], BF16, name="wp_sb")
         w2_sb = held.tile([D, D], BF16, name="w2_sb")
         b1_sb = held.tile([D, 1], F32, name="b1_sb")
-        b2_sb = held.tile([D, 1], F32, name="b2_sb")
-        ctx_sb = held.tile([D, 1], F32, name="ctx_sb")
+        ctx_row = held.tile([1, D], F32, name="ctx_row")
+        b2_rows = held.tile([D, D], F32, name="b2_rows")
 
+        nc.gpsimd.memset(b2_rows[:], 0.0)
+        nc.gpsimd.dma_start(b2_rows[0:D:GROUP, :], b2.rearrange("r o -> (r o)").partition_broadcast(GROUPS))
+        nc.sync.dma_start(ctx_row[:], ctx.rearrange("r o -> o r"))
         nc.sync.dma_start(offsets[:], offs)
         nc.sync.dma_start(table_sb[:], table)
         nc.sync.dma_start(qpu_sb[:], qpu)
-        nc.sync.dma_start(w2_sb[:], w2)
-        nc.sync.dma_start(b2_sb[:], b2)
         nc.scalar.dma_start(wq_sb[:], wq)
+        nc.scalar.dma_start(w2_sb[:], w2)
         nc.scalar.dma_start(wp_sb[:], wp)
         nc.scalar.dma_start(b1_sb[:], b1)
-        nc.scalar.dma_start(ctx_sb[:], ctx)
 
         zeros = held.tile([D, D], BF16, name="zeros")
         nc.vector.memset(zeros[:], 0.0)
+        ones_row = held.tile([1, D], F32, name="ones_row")
+        nc.vector.memset(ones_row[:], 1.0)
         primed = held.tile([D, 1], F32, name="primed")
         nc.scalar.activation(primed[:], zeros[:, 0:1], IDENTITY)
         unread = layer1.tile([D, S], F32, name="unread", tag="pre")
         for turn in range(WARM):
             nc.tensor.matmul(unread[:], zeros[:], zeros[:, 0:1].to_broadcast([D, S]), start=True, stop=True)
+
+        ctx_rows = folded.tile([D, D], F32, name="ctx_rows")
+        nc.tensor.matmul(ctx_rows[:], ones_row[:], ctx_row[:], start=True, stop=True)
+        products = held.tile([D, D], F32, name="products")
+        v_sb = held.tile([D, 1], F32, name="v_sb")
+        nc.vector.scalar_tensor_tensor(products[:], w2_sb[:], 1.0, ctx_rows[:], MULT, MULT, accum_out=v_sb[:])
 
         def bias_relu(i, h_i, pre_i):
             if i % 2 == 0:
@@ -57,17 +69,11 @@ def tile_policynetwork_kernel(tc, table, qpu, wq, wp, b1, w2, b2, ctx, offs, out
             else:
                 nc.scalar.activation(h_i, pre_i, RELU, bias=b1_sb[:])
 
-        def add_b2(i, keys_i, keys_ps_i):
+        def add_c(i, logits_i, sums_i):
             if i % 2 == 0:
-                nc.vector.tensor_scalar_add(keys_i, keys_ps_i, b2_sb[:])
+                nc.vector.tensor_scalar_add(logits_i, sums_i, c_sb[:])
             else:
-                nc.scalar.activation(keys_i, keys_ps_i, IDENTITY, bias=b2_sb[:])
-
-        def copy_out(i, logits_i, sums_i):
-            if i % 2 == 0:
-                nc.vector.tensor_copy(logits_i, sums_i)
-            else:
-                nc.scalar.activation(logits_i, sums_i, IDENTITY)
+                nc.scalar.activation(logits_i, sums_i, IDENTITY, bias=c_sb[:])
 
         pre = []
         for i in range(PIECES):
@@ -78,21 +84,26 @@ def tile_policynetwork_kernel(tc, table, qpu, wq, wp, b1, w2, b2, ctx, offs, out
         h = []
         for i in range(PIECES):
             nc.tensor.matmul(pre[i][:], wp_sb[:], qpu_sb[:, i * PIECE : (i + 1) * PIECE], start=False, stop=True)
-            h.append(work.tile([D, PIECE], BF16, name="h"))
+            h.append(work.tile([D, PIECE], F32, name="h"))
             bias_relu(i, h[i][:], pre[i][:])
 
-        keys = []
+        v_group = v_sb[:, 0:1].to_broadcast([D, GROUP])
+        c_sb = held.tile([D, 1], F32, name="c_sb")
+        nc.vector.scalar_tensor_tensor(products[:], b2_rows[:], 1.0, ctx_rows[:], MULT, MULT, accum_out=c_sb[:])
         for i in range(PIECES):
-            keys_ps = layer2.tile([D, PIECE], F32, name="keys_ps")
-            nc.tensor.matmul(keys_ps[:], w2_sb[:], h[i][:], start=True, stop=True)
-            keys.append(work.tile([D, PIECE], F32, name="keys"))
-            add_b2(i, keys[i][:], keys_ps[:])
-
-        logits = held.tile([D, PIECE], F32, name="logits")
-        for i in range(PIECES):
-            sums = layer1.tile([D, PIECE], F32, name="sums", tag="pre")
-            row = slice(i * GROUP, i * GROUP + 1)
-            nc.tensor.matmul(sums[row, :], ctx_sb[:], keys[i][:], start=True, stop=True)
-            copy_out(i, logits[row, :], sums[row, :])
+            sums = summed.tile([D, SHARE], F32, name="sums")
+            for g in range(GROUPS):
+                nc.tensor.matmul(
+                    sums[g * GROUP : (g + 1) * GROUP, :],
+                    v_group,
+                    h[i][:, g * SHARE : (g + 1) * SHARE],
+                    start=True,
+                    stop=True,
+                )
+            logits = work.tile([D, SHARE], F32, name="logits")
+            add_c(i, logits[:], sums[:])
             queue = nc.sync if i % 2 == 0 else nc.scalar
-            queue.dma_start(out[:, i * PIECE : (i + 1) * PIECE], logits[row, :])
+            queue.dma_start(
+                out[:, i * PIECE : (i + 1) * PIECE].rearrange("o (g x) -> (o g) x", g=GROUPS),
+                logits[0:D:GROUP, :],
+            )

@@ -37,7 +37,6 @@ def tile_policynetwork_kernel(tc, table, qpu, wq, wp, b1, w2, b2, ctx, offs, out
         b2_rows = held.tile([D, D], F32, name="b2_rows")
 
         nc.gpsimd.memset(b2_rows[:], 0.0)
-        nc.gpsimd.dma_start(b2_rows[0:D:GROUP, :], b2.rearrange("r o -> (r o)").partition_broadcast(GROUPS))
         nc.sync.dma_start(ctx_row[:], ctx.rearrange("r o -> o r"))
         nc.sync.dma_start(offsets[:], offs)
         nc.sync.dma_start(table_sb[:], table)
@@ -46,6 +45,7 @@ def tile_policynetwork_kernel(tc, table, qpu, wq, wp, b1, w2, b2, ctx, offs, out
         nc.scalar.dma_start(w2_sb[:], w2)
         nc.scalar.dma_start(wp_sb[:], wp)
         nc.scalar.dma_start(b1_sb[:], b1)
+        nc.sync.dma_start(b2_rows[0:D:GROUP, :], b2.rearrange("r o -> (r o)").partition_broadcast(GROUPS))
 
         zeros = held.tile([D, D], BF16, name="zeros")
         nc.vector.memset(zeros[:], 0.0)

@@ -11,7 +11,8 @@ PIECES = 4
 PIECE = N // PIECES
 GROUP = 32
 GROUPS = D // GROUP
-SHARE = PIECE // GROUPS
+PAIR = 2 * PIECE
+SHARE = PAIR // GROUPS
 WARM = 3
 
 FLOPS = 2 * D * D * N * 2 + 2 * D * D + 2 * D + 2 * D * N
@@ -24,7 +25,7 @@ def tile_policynetwork_kernel(tc, table, qpu, wq, wp, b1, w2, b2, ctx, offs, out
         tc.tile_pool(name="work", bufs=PIECES) as work,
         tc.psum_pool(name="layer1", bufs=PIECES) as layer1,
         tc.psum_pool(name="folded", bufs=1) as folded,
-        tc.psum_pool(name="summed", bufs=3) as summed,
+        tc.psum_pool(name="summed", bufs=2) as summed,
     ):
         offsets = held.tile([D, N // 16], U16, name="offsets")
         table_sb = held.tile([D, S], BF16, name="table_sb")
@@ -37,25 +38,25 @@ def tile_policynetwork_kernel(tc, table, qpu, wq, wp, b1, w2, b2, ctx, offs, out
         b2_rows = held.tile([D, D], F32, name="b2_rows")
 
         nc.gpsimd.memset(b2_rows[:], 0.0)
-        nc.sync.dma_start(ctx_row[:], ctx.rearrange("r o -> o r"))
-        nc.sync.dma_start(offsets[:], offs)
         nc.sync.dma_start(table_sb[:], table)
+        nc.sync.dma_start(offsets[:], offs)
         nc.sync.dma_start(qpu_sb[:], qpu)
+        nc.sync.dma_start(wp_sb[:], wp)
+        nc.scalar.dma_start(ctx_row[:], ctx.rearrange("r o -> o r"))
         nc.scalar.dma_start(wq_sb[:], wq)
         nc.scalar.dma_start(w2_sb[:], w2)
-        nc.scalar.dma_start(wp_sb[:], wp)
         nc.scalar.dma_start(b1_sb[:], b1)
         nc.sync.dma_start(b2_rows[0:D:GROUP, :], b2.rearrange("r o -> (r o)").partition_broadcast(GROUPS))
 
-        zeros = held.tile([D, D], BF16, name="zeros")
+        zeros = held.tile([D, 1], BF16, name="zeros")
         nc.vector.memset(zeros[:], 0.0)
         ones_row = held.tile([1, D], F32, name="ones_row")
         nc.vector.memset(ones_row[:], 1.0)
         primed = held.tile([D, 1], F32, name="primed")
-        nc.scalar.activation(primed[:], zeros[:, 0:1], IDENTITY)
+        nc.scalar.activation(primed[:], zeros[:], IDENTITY)
         unread = layer1.tile([D, S], F32, name="unread", tag="pre")
         for turn in range(WARM):
-            nc.tensor.matmul(unread[:], zeros[:], zeros[:, 0:1].to_broadcast([D, S]), start=True, stop=True)
+            nc.tensor.matmul(unread[:], zeros[:].to_broadcast([D, D]), zeros[:].to_broadcast([D, S]), start=True, stop=True)
 
         ctx_rows = folded.tile([D, D], F32, name="ctx_rows")
         nc.tensor.matmul(ctx_rows[:], ones_row[:], ctx_row[:], start=True, stop=True)
@@ -90,20 +91,21 @@ def tile_policynetwork_kernel(tc, table, qpu, wq, wp, b1, w2, b2, ctx, offs, out
         v_group = v_sb[:, 0:1].to_broadcast([D, GROUP])
         c_sb = held.tile([D, 1], F32, name="c_sb")
         nc.vector.scalar_tensor_tensor(products[:], b2_rows[:], 1.0, ctx_rows[:], MULT, MULT, accum_out=c_sb[:])
-        for i in range(PIECES):
+        for pair in range(N // PAIR):
             sums = summed.tile([D, SHARE], F32, name="sums")
             for g in range(GROUPS):
+                i, half = 2 * pair + g // 2, g % 2
                 nc.tensor.matmul(
                     sums[g * GROUP : (g + 1) * GROUP, :],
                     v_group,
-                    h[i][:, g * SHARE : (g + 1) * SHARE],
+                    h[i][:, half * SHARE : (half + 1) * SHARE],
                     start=True,
                     stop=True,
                 )
             logits = work.tile([D, SHARE], F32, name="logits")
-            add_c(i, logits[:], sums[:])
-            queue = nc.sync if i % 2 == 0 else nc.scalar
+            add_c(pair, logits[:], sums[:])
+            queue = nc.sync if pair % 2 == 0 else nc.scalar
             queue.dma_start(
-                out[:, i * PIECE : (i + 1) * PIECE].rearrange("o (g x) -> (o g) x", g=GROUPS),
+                out[:, pair * PAIR : (pair + 1) * PAIR].rearrange("o (g x) -> (o g) x", g=GROUPS),
                 logits[0:D:GROUP, :],
             )

@@ -56,7 +56,14 @@ def tile_policynetwork_kernel(tc, table, qpu, wq, wp, b1, w2, b2, ctx, offs, out
         nc.scalar.activation(primed[:], zeros[:], IDENTITY)
         unread = layer1.tile([D, S], F32, name="unread", tag="pre")
         for turn in range(WARM):
-            nc.tensor.matmul(unread[:], zeros[:].to_broadcast([D, D]), zeros[:].to_broadcast([D, S]), start=True, stop=True)
+            for g in range(GROUPS):
+                nc.tensor.matmul(
+                    unread[g * GROUP : (g + 1) * GROUP, :],
+                    zeros[:].to_broadcast([D, GROUP]),
+                    zeros[:].to_broadcast([D, S]),
+                    start=True,
+                    stop=True,
+                )
 
         ctx_rows = folded.tile([D, D], F32, name="ctx_rows")
         nc.tensor.matmul(ctx_rows[:], ones_row[:], ctx_row[:], start=True, stop=True)

@@ -3,6 +3,7 @@ import concourse.mybir as mybir
 BF16, F32, U16 = mybir.dt.bfloat16, mybir.dt.float32, mybir.dt.uint16
 IDENTITY, RELU = mybir.ActivationFunctionType.Identity, mybir.ActivationFunctionType.Relu
 ADD, MAX, MULT = mybir.AluOpType.add, mybir.AluOpType.max, mybir.AluOpType.mult
+SUBTRACT = mybir.AluOpType.subtract
 
 D = 128
 S = 512
@@ -70,6 +71,10 @@ def tile_policynetwork_kernel(tc, table, qpu, wq, wp, b1, w2, b2, ctx, offs, out
         products = held.tile([D, D], F32, name="products")
         v_sb = held.tile([D, 1], F32, name="v_sb")
         nc.vector.scalar_tensor_tensor(products[:], w2_sb[:], 1.0, ctx_rows[:], MULT, MULT, accum_out=v_sb[:])
+        v_high = held.tile([D, 1], BF16, name="v_high")
+        v_low = held.tile([D, 1], BF16, name="v_low")
+        nc.vector.tensor_copy(v_high[:], v_sb[:])
+        nc.vector.tensor_tensor(v_low[:], v_sb[:], v_high[:], SUBTRACT)
 
         def bias_relu(i, h_i, pre_i):
             if i % 2 == 0:
@@ -92,23 +97,23 @@ def tile_policynetwork_kernel(tc, table, qpu, wq, wp, b1, w2, b2, ctx, offs, out
         h = []
         for i in range(PIECES):
             nc.tensor.matmul(pre[i][:], wp_sb[:], qpu_sb[:, i * PIECE : (i + 1) * PIECE], start=False, stop=True)
-            h.append(work.tile([D, PIECE], F32, name="h"))
+            h.append(work.tile([D, PIECE], BF16, name="h"))
             bias_relu(i, h[i][:], pre[i][:])
 
-        v_group = v_sb[:, 0:1].to_broadcast([D, GROUP])
         c_sb = held.tile([D, 1], F32, name="c_sb")
         nc.vector.scalar_tensor_tensor(products[:], b2_rows[:], 1.0, ctx_rows[:], MULT, MULT, accum_out=c_sb[:])
         for pair in range(N // PAIR):
             sums = summed.tile([D, SHARE], F32, name="sums")
-            for g in range(GROUPS):
-                i, half = 2 * pair + g // 2, g % 2
-                nc.tensor.matmul(
-                    sums[g * GROUP : (g + 1) * GROUP, :],
-                    v_group,
-                    h[i][:, half * SHARE : (half + 1) * SHARE],
-                    start=True,
-                    stop=True,
-                )
+            for step, part in enumerate((v_high, v_low)):
+                for g in range(GROUPS):
+                    i, half = 2 * pair + g // 2, g % 2
+                    nc.tensor.matmul(
+                        sums[g * GROUP : (g + 1) * GROUP, :],
+                        part[:].to_broadcast([D, GROUP]),
+                        h[i][:, half * SHARE : (half + 1) * SHARE],
+                        start=step == 0,
+                        stop=step == 1,
+                    )
             logits = work.tile([D, SHARE], F32, name="logits")
             add_c(pair, logits[:], sums[:])
             queue = nc.sync if pair % 2 == 0 else nc.scalar

@@ -25,7 +25,6 @@ def tile_policynetwork_kernel(tc, table, qpu, wq, wp, b1, w2, b2, ctx, offs, out
         tc.tile_pool(name="held", bufs=1) as held,
         tc.tile_pool(name="work", bufs=PIECES) as work,
         tc.psum_pool(name="layer1", bufs=PIECES) as layer1,
-        tc.psum_pool(name="folded", bufs=1) as folded,
         tc.psum_pool(name="summed", bufs=2) as summed,
     ):
         offsets = held.tile([D, N // 16], U16, name="offsets")
@@ -35,24 +34,23 @@ def tile_policynetwork_kernel(tc, table, qpu, wq, wp, b1, w2, b2, ctx, offs, out
         wp_sb = held.tile([D, D], BF16, name="wp_sb")
         w2_sb = held.tile([D, D], BF16, name="w2_sb")
         b1_sb = held.tile([D, 1], F32, name="b1_sb")
-        ctx_row = held.tile([1, D], F32, name="ctx_row")
-        b2_rows = held.tile([D, D], F32, name="b2_rows")
-
-        nc.gpsimd.memset(b2_rows[:], 0.0)
-        nc.sync.dma_start(table_sb[:], table)
-        nc.sync.dma_start(offsets[:], offs)
-        nc.sync.dma_start(qpu_sb[:], qpu)
-        nc.sync.dma_start(wp_sb[:], wp)
-        nc.scalar.dma_start(ctx_row[:], ctx.rearrange("r o -> o r"))
-        nc.scalar.dma_start(wq_sb[:], wq)
-        nc.scalar.dma_start(w2_sb[:], w2)
-        nc.scalar.dma_start(b1_sb[:], b1)
-        nc.sync.dma_start(b2_rows[0:D:GROUP, :], b2.rearrange("r o -> (r o)").partition_broadcast(GROUPS))
+        ctx_firsts = held.tile([D, D], F32, name="ctx_firsts", align_bytes=64)
+        b2_firsts = held.tile([D, D], F32, name="b2_firsts")
 
         zeros = held.tile([D, 1], BF16, name="zeros")
         nc.vector.memset(zeros[:], 0.0)
-        ones_row = held.tile([1, D], F32, name="ones_row")
-        nc.vector.memset(ones_row[:], 1.0)
+        nc.vector.memset(ctx_firsts[:], 0.0)
+        nc.gpsimd.memset(b2_firsts[:], 0.0)
+        nc.sync.dma_start(table_sb[:], table)
+        nc.sync.dma_start(offsets[:], offs)
+        nc.sync.dma_start(ctx_firsts[0:D:GROUP, :], ctx.rearrange("r o -> (r o)").partition_broadcast(GROUPS))
+        nc.sync.dma_start(qpu_sb[:], qpu)
+        nc.sync.dma_start(wp_sb[:], wp)
+        nc.scalar.dma_start(wq_sb[:], wq)
+        nc.scalar.dma_start(w2_sb[:], w2)
+        nc.scalar.dma_start(b1_sb[:], b1)
+        nc.sync.dma_start(b2_firsts[0:D:GROUP, :], b2.rearrange("r o -> (r o)").partition_broadcast(GROUPS))
+
         primed = held.tile([D, 1], F32, name="primed")
         nc.scalar.activation(primed[:], zeros[:], IDENTITY)
         unread = layer1.tile([D, S], F32, name="unread", tag="pre")
@@ -66,8 +64,15 @@ def tile_policynetwork_kernel(tc, table, qpu, wq, wp, b1, w2, b2, ctx, offs, out
                     stop=True,
                 )
 
-        ctx_rows = folded.tile([D, D], F32, name="ctx_rows")
-        nc.tensor.matmul(ctx_rows[:], ones_row[:], ctx_row[:], start=True, stop=True)
+        turned = held.tile([D, D], F32, name="turned", align_bytes=64)
+        nc.vector.transpose(turned[:], ctx_firsts[:])
+        repeated = held.tile([D, D], F32, name="repeated", align_bytes=64)
+        nc.vector.tensor_copy(
+            repeated[:].rearrange("p (b j) -> p b j", j=GROUP),
+            turned[:].rearrange("p (b j) -> p b j", j=GROUP)[:, :, 0:1].to_broadcast([D, GROUPS, GROUP]),
+        )
+        ctx_rows = held.tile([D, D], F32, name="ctx_rows", align_bytes=64)
+        nc.vector.transpose(ctx_rows[:], repeated[:])
         products = held.tile([D, D], F32, name="products")
         v_sb = held.tile([D, 1], F32, name="v_sb")
         nc.vector.scalar_tensor_tensor(products[:], w2_sb[:], 1.0, ctx_rows[:], MULT, MULT, accum_out=v_sb[:])
@@ -101,7 +106,7 @@ def tile_policynetwork_kernel(tc, table, qpu, wq, wp, b1, w2, b2, ctx, offs, out
             bias_relu(i, h[i][:], pre[i][:])
 
         c_sb = held.tile([D, 1], F32, name="c_sb")
-        nc.vector.scalar_tensor_tensor(products[:], b2_rows[:], 1.0, ctx_rows[:], MULT, MULT, accum_out=c_sb[:])
+        nc.vector.scalar_tensor_tensor(products[:], b2_firsts[:], 1.0, ctx_rows[:], MULT, MULT, accum_out=c_sb[:])
         for pair in range(N // PAIR):
             sums = summed.tile([D, SHARE], F32, name="sums")
             for step, part in enumerate((v_high, v_low)):

@@ -3,7 +3,6 @@ import concourse.mybir as mybir
 BF16, F32, U16 = mybir.dt.bfloat16, mybir.dt.float32, mybir.dt.uint16
 IDENTITY, RELU = mybir.ActivationFunctionType.Identity, mybir.ActivationFunctionType.Relu
 ADD, MAX, MULT = mybir.AluOpType.add, mybir.AluOpType.max, mybir.AluOpType.mult
-SUBTRACT = mybir.AluOpType.subtract
 
 D = 128
 S = 512
@@ -37,9 +36,7 @@ def tile_policynetwork_kernel(tc, table, qpu, wq, wp, b1, w2, b2, ctx, offs, out
         ctx_firsts = held.tile([D, D], F32, name="ctx_firsts", align_bytes=64)
         b2_firsts = held.tile([D, D], F32, name="b2_firsts")
 
-        zeros = held.tile([D, 1], BF16, name="zeros")
-        nc.vector.memset(zeros[:], 0.0)
-        nc.vector.memset(ctx_firsts[:], 0.0)
+        nc.gpsimd.memset(ctx_firsts[:], 0.0)
         nc.gpsimd.memset(b2_firsts[:], 0.0)
         nc.sync.dma_start(table_sb[:], table)
         nc.sync.dma_start(offsets[:], offs)
@@ -51,6 +48,8 @@ def tile_policynetwork_kernel(tc, table, qpu, wq, wp, b1, w2, b2, ctx, offs, out
         nc.scalar.dma_start(b1_sb[:], b1)
         nc.sync.dma_start(b2_firsts[0:D:GROUP, :], b2.rearrange("r o -> (r o)").partition_broadcast(GROUPS))
 
+        zeros = held.tile([D, 1], BF16, name="zeros")
+        nc.vector.memset(zeros[:], 0.0)
         primed = held.tile([D, 1], F32, name="primed")
         nc.scalar.activation(primed[:], zeros[:], IDENTITY)
         unread = layer1.tile([D, S], F32, name="unread", tag="pre")
@@ -76,10 +75,6 @@ def tile_policynetwork_kernel(tc, table, qpu, wq, wp, b1, w2, b2, ctx, offs, out
         products = held.tile([D, D], F32, name="products")
         v_sb = held.tile([D, 1], F32, name="v_sb")
         nc.vector.scalar_tensor_tensor(products[:], w2_sb[:], 1.0, ctx_rows[:], MULT, MULT, accum_out=v_sb[:])
-        v_high = held.tile([D, 1], BF16, name="v_high")
-        v_low = held.tile([D, 1], BF16, name="v_low")
-        nc.vector.tensor_copy(v_high[:], v_sb[:])
-        nc.vector.tensor_tensor(v_low[:], v_sb[:], v_high[:], SUBTRACT)
 
         def bias_relu(i, h_i, pre_i):
             if i % 2 == 0:
@@ -102,23 +97,22 @@ def tile_policynetwork_kernel(tc, table, qpu, wq, wp, b1, w2, b2, ctx, offs, out
         h = []
         for i in range(PIECES):
             nc.tensor.matmul(pre[i][:], wp_sb[:], qpu_sb[:, i * PIECE : (i + 1) * PIECE], start=False, stop=True)
-            h.append(work.tile([D, PIECE], BF16, name="h"))
+            h.append(work.tile([D, PIECE], F32, name="h"))
             bias_relu(i, h[i][:], pre[i][:])
 
         c_sb = held.tile([D, 1], F32, name="c_sb")
         nc.vector.scalar_tensor_tensor(products[:], b2_firsts[:], 1.0, ctx_rows[:], MULT, MULT, accum_out=c_sb[:])
         for pair in range(N // PAIR):
             sums = summed.tile([D, SHARE], F32, name="sums")
-            for step, part in enumerate((v_high, v_low)):
-                for g in range(GROUPS):
-                    i, half = 2 * pair + g // 2, g % 2
-                    nc.tensor.matmul(
-                        sums[g * GROUP : (g + 1) * GROUP, :],
-                        part[:].to_broadcast([D, GROUP]),
-                        h[i][:, half * SHARE : (half + 1) * SHARE],
-                        start=step == 0,
-                        stop=step == 1,
-                    )
+            for g in range(GROUPS):
+                i, half = 2 * pair + g // 2, g % 2
+                nc.tensor.matmul(
+                    sums[g * GROUP : (g + 1) * GROUP, :],
+                    v_sb[:].to_broadcast([D, GROUP]),
+                    h[i][:, half * SHARE : (half + 1) * SHARE],
+                    start=True,
+                    stop=True,
+                )
             logits = work.tile([D, SHARE], F32, name="logits")
             add_c(pair, logits[:], sums[:])
             queue = nc.sync if pair % 2 == 0 else nc.scalar

@@ -3,6 +3,7 @@ import concourse.mybir as mybir
 BF16, F32, U16 = mybir.dt.bfloat16, mybir.dt.float32, mybir.dt.uint16
 IDENTITY, RELU = mybir.ActivationFunctionType.Identity, mybir.ActivationFunctionType.Relu
 ADD, MAX, MULT = mybir.AluOpType.add, mybir.AluOpType.max, mybir.AluOpType.mult
+IS_EQUAL = mybir.AluOpType.is_equal
 
 D = 128
 S = 512
@@ -24,6 +25,7 @@ def tile_policynetwork_kernel(tc, table, qpu, wq, wp, b1, w2, b2, ctx, offs, out
         tc.tile_pool(name="held", bufs=1) as held,
         tc.tile_pool(name="work", bufs=PIECES) as work,
         tc.psum_pool(name="layer1", bufs=PIECES) as layer1,
+        tc.psum_pool(name="spread", bufs=1) as spread,
         tc.psum_pool(name="summed", bufs=2) as summed,
     ):
         offsets = held.tile([D, N // 16], U16, name="offsets")
@@ -33,23 +35,33 @@ def tile_policynetwork_kernel(tc, table, qpu, wq, wp, b1, w2, b2, ctx, offs, out
         wp_sb = held.tile([D, D], BF16, name="wp_sb")
         w2_sb = held.tile([D, D], BF16, name="w2_sb")
         b1_sb = held.tile([D, 1], F32, name="b1_sb")
-        ctx_firsts = held.tile([D, D], F32, name="ctx_firsts", align_bytes=64)
+        ctx_sb = held.tile([D, 1], F32, name="ctx_sb")
         b2_firsts = held.tile([D, D], F32, name="b2_firsts")
 
-        nc.gpsimd.memset(ctx_firsts[:], 0.0)
+        identity = held.tile([D, D], F32, name="identity")
+        nc.gpsimd.memset(identity[:], 0.0)
         nc.gpsimd.memset(b2_firsts[:], 0.0)
         nc.sync.dma_start(table_sb[:], table)
         nc.sync.dma_start(offsets[:], offs)
-        nc.sync.dma_start(ctx_firsts[0:D:GROUP, :], ctx.rearrange("r o -> (r o)").partition_broadcast(GROUPS))
         nc.sync.dma_start(qpu_sb[:], qpu)
         nc.sync.dma_start(wp_sb[:], wp)
         nc.scalar.dma_start(wq_sb[:], wq)
+        nc.scalar.dma_start(ctx_sb[:], ctx)
         nc.scalar.dma_start(w2_sb[:], w2)
         nc.scalar.dma_start(b1_sb[:], b1)
         nc.sync.dma_start(b2_firsts[0:D:GROUP, :], b2.rearrange("r o -> (r o)").partition_broadcast(GROUPS))
 
         zeros = held.tile([D, 1], BF16, name="zeros")
         nc.vector.memset(zeros[:], 0.0)
+        ones = held.tile([D, GROUP], F32, name="ones")
+        nc.vector.memset(ones[:], 1.0)
+        column_number = held.tile([D, GROUP], F32, name="column_number", align_bytes=64)
+        nc.vector.tensor_tensor_scan(column_number[:], ones[:], ones[:], 0.0, MULT, ADD)
+        row_number = held.tile([D, GROUP], F32, name="row_number", align_bytes=64)
+        nc.vector.transpose(row_number[:], column_number[:])
+        for g in range(GROUPS):
+            block = slice(g * GROUP, (g + 1) * GROUP)
+            nc.vector.tensor_tensor(identity[block, block], row_number[block, :], column_number[block, :], IS_EQUAL)
         primed = held.tile([D, 1], F32, name="primed")
         nc.scalar.activation(primed[:], zeros[:], IDENTITY)
         unread = layer1.tile([D, S], F32, name="unread", tag="pre")
@@ -63,15 +75,15 @@ def tile_policynetwork_kernel(tc, table, qpu, wq, wp, b1, w2, b2, ctx, offs, out
                     stop=True,
                 )
 
-        turned = held.tile([D, D], F32, name="turned", align_bytes=64)
-        nc.vector.transpose(turned[:], ctx_firsts[:])
-        repeated = held.tile([D, D], F32, name="repeated", align_bytes=64)
-        nc.vector.tensor_copy(
-            repeated[:].rearrange("p (b j) -> p b j", j=GROUP),
-            turned[:].rearrange("p (b j) -> p b j", j=GROUP)[:, :, 0:1].to_broadcast([D, GROUPS, GROUP]),
-        )
-        ctx_rows = held.tile([D, D], F32, name="ctx_rows", align_bytes=64)
-        nc.vector.transpose(ctx_rows[:], repeated[:])
+        pre = []
+        ctx_rows = spread.tile([D, D], F32, name="ctx_rows")
+        for i in range(PIECES):
+            pre.append(layer1.tile([D, PIECE], F32, name="pre"))
+            entries = offsets[:, i * (PIECE // 16) : (i + 1) * (PIECE // 16)]
+            nc.tensor.matmul(pre[i][:], wq_sb[:], table_sb[:].indirect(entries), start=True, stop=False)
+            if i == PIECES // 2 - 1:
+                nc.tensor.transpose(ctx_rows[:], ctx_sb[:].to_broadcast([D, D]), identity[:])
+
         products = held.tile([D, D], F32, name="products")
         v_sb = held.tile([D, 1], F32, name="v_sb")
         nc.vector.scalar_tensor_tensor(products[:], w2_sb[:], 1.0, ctx_rows[:], MULT, MULT, accum_out=v_sb[:])
@@ -87,12 +99,6 @@ def tile_policynetwork_kernel(tc, table, qpu, wq, wp, b1, w2, b2, ctx, offs, out
                 nc.vector.tensor_scalar_add(logits_i, sums_i, c_sb[:])
             else:
                 nc.scalar.activation(logits_i, sums_i, IDENTITY, bias=c_sb[:])
-
-        pre = []
-        for i in range(PIECES):
-            pre.append(layer1.tile([D, PIECE], F32, name="pre"))
-            entries = offsets[:, i * (PIECE // 16) : (i + 1) * (PIECE // 16)]
-            nc.tensor.matmul(pre[i][:], wq_sb[:], table_sb[:].indirect(entries), start=True, stop=False)
 
         h = []
         for i in range(PIECES):

@@ -3,7 +3,7 @@ import concourse.mybir as mybir
 BF16, F32, U16 = mybir.dt.bfloat16, mybir.dt.float32, mybir.dt.uint16
 IDENTITY, RELU = mybir.ActivationFunctionType.Identity, mybir.ActivationFunctionType.Relu
 ADD, MAX, MULT = mybir.AluOpType.add, mybir.AluOpType.max, mybir.AluOpType.mult
-IS_EQUAL = mybir.AluOpType.is_equal
+SUBTRACT, IS_EQUAL = mybir.AluOpType.subtract, mybir.AluOpType.is_equal
 
 D = 128
 S = 512
@@ -81,12 +81,16 @@ def tile_policynetwork_kernel(tc, table, qpu, wq, wp, b1, w2, b2, ctx, offs, out
             pre.append(layer1.tile([D, PIECE], F32, name="pre"))
             entries = offsets[:, i * (PIECE // 16) : (i + 1) * (PIECE // 16)]
             nc.tensor.matmul(pre[i][:], wq_sb[:], table_sb[:].indirect(entries), start=True, stop=False)
-            if i == PIECES // 2 - 1:
+            if i == 0:
                 nc.tensor.transpose(ctx_rows[:], ctx_sb[:].to_broadcast([D, D]), identity[:])
 
         products = held.tile([D, D], F32, name="products")
         v_sb = held.tile([D, 1], F32, name="v_sb")
         nc.vector.scalar_tensor_tensor(products[:], w2_sb[:], 1.0, ctx_rows[:], MULT, MULT, accum_out=v_sb[:])
+        v_high = held.tile([D, 1], BF16, name="v_high")
+        v_low = held.tile([D, 1], BF16, name="v_low")
+        nc.vector.tensor_copy(v_high[:], v_sb[:])
+        nc.vector.tensor_tensor(v_low[:], v_sb[:], v_high[:], SUBTRACT)
 
         def bias_relu(i, h_i, pre_i):
             if i % 2 == 0:
@@ -103,22 +107,23 @@ def tile_policynetwork_kernel(tc, table, qpu, wq, wp, b1, w2, b2, ctx, offs, out
         h = []
         for i in range(PIECES):
             nc.tensor.matmul(pre[i][:], wp_sb[:], qpu_sb[:, i * PIECE : (i + 1) * PIECE], start=False, stop=True)
-            h.append(work.tile([D, PIECE], F32, name="h"))
+            h.append(work.tile([D, PIECE], BF16, name="h"))
             bias_relu(i, h[i][:], pre[i][:])
 
         c_sb = held.tile([D, 1], F32, name="c_sb")
         nc.vector.scalar_tensor_tensor(products[:], b2_firsts[:], 1.0, ctx_rows[:], MULT, MULT, accum_out=c_sb[:])
         for pair in range(N // PAIR):
             sums = summed.tile([D, SHARE], F32, name="sums")
-            for g in range(GROUPS):
-                i, half = 2 * pair + g // 2, g % 2
-                nc.tensor.matmul(
-                    sums[g * GROUP : (g + 1) * GROUP, :],
-                    v_sb[:].to_broadcast([D, GROUP]),
-                    h[i][:, half * SHARE : (half + 1) * SHARE],
-                    start=True,
-                    stop=True,
-                )
+            for step, part in enumerate((v_high, v_low)):
+                for g in range(GROUPS):
+                    i, half = 2 * pair + g // 2, g % 2
+                    nc.tensor.matmul(
+                        sums[g * GROUP : (g + 1) * GROUP, :],
+                        part[:].to_broadcast([D, GROUP]),
+                        h[i][:, half * SHARE : (half + 1) * SHARE],
+                        start=step == 0,
+                        stop=step == 1,
+                    )
             logits = work.tile([D, SHARE], F32, name="logits")
             add_c(pair, logits[:], sums[:])
             queue = nc.sync if pair % 2 == 0 else nc.scalar

import concourse.mybir as mybir

BF16, F32, U16 = mybir.dt.bfloat16, mybir.dt.float32, mybir.dt.uint16
IDENTITY, RELU = mybir.ActivationFunctionType.Identity, mybir.ActivationFunctionType.Relu
ADD, MAX, MULT = mybir.AluOpType.add, mybir.AluOpType.max, mybir.AluOpType.mult
SUBTRACT, IS_EQUAL = mybir.AluOpType.subtract, mybir.AluOpType.is_equal

D = 128
S = 512
N = 1024
PIECES = 4
PIECE = N // PIECES
GROUP = 32
GROUPS = D // GROUP
PAIR = 2 * PIECE
SHARE = PAIR // GROUPS
WARM = 3

FLOPS = 2 * D * D * N * 2 + 2 * D * D + 2 * D + 2 * D * N


def tile_policynetwork_kernel(tc, table, qpu, wq, wp, b1, w2, b2, ctx, offs, out):
    nc = tc.nc
    with (
        tc.tile_pool(name="held", bufs=1) as held,
        tc.tile_pool(name="work", bufs=PIECES) as work,
        tc.psum_pool(name="layer1", bufs=PIECES) as layer1,
        tc.psum_pool(name="spread", bufs=1) as spread,
        tc.psum_pool(name="summed", bufs=2) as summed,
    ):
        offsets = held.tile([D, N // 16], U16, name="offsets")
        table_sb = held.tile([D, S], BF16, name="table_sb")
        qpu_sb = held.tile([D, N], BF16, name="qpu_sb")
        wq_sb = held.tile([D, D], BF16, name="wq_sb")
        wp_sb = held.tile([D, D], BF16, name="wp_sb")
        w2_sb = held.tile([D, D], BF16, name="w2_sb")
        b1_sb = held.tile([D, 1], F32, name="b1_sb")
        ctx_sb = held.tile([D, 1], F32, name="ctx_sb")
        b2_firsts = held.tile([D, D], F32, name="b2_firsts")

        identity = held.tile([D, D], F32, name="identity")
        nc.gpsimd.memset(identity[:], 0.0)
        nc.gpsimd.memset(b2_firsts[:], 0.0)
        nc.sync.dma_start(table_sb[:], table)
        nc.sync.dma_start(offsets[:], offs)
        nc.sync.dma_start(qpu_sb[:], qpu)
        nc.sync.dma_start(wp_sb[:], wp)
        nc.scalar.dma_start(wq_sb[:], wq)
        nc.scalar.dma_start(ctx_sb[:], ctx)
        nc.scalar.dma_start(w2_sb[:], w2)
        nc.scalar.dma_start(b1_sb[:], b1)
        nc.sync.dma_start(b2_firsts[0:D:GROUP, :], b2.rearrange("r o -> (r o)").partition_broadcast(GROUPS))

        zeros = held.tile([D, 1], BF16, name="zeros")
        nc.vector.memset(zeros[:], 0.0)
        ones = held.tile([D, GROUP], F32, name="ones")
        nc.vector.memset(ones[:], 1.0)
        column_number = held.tile([D, GROUP], F32, name="column_number", align_bytes=64)
        nc.vector.tensor_tensor_scan(column_number[:], ones[:], ones[:], 0.0, MULT, ADD)
        row_number = held.tile([D, GROUP], F32, name="row_number", align_bytes=64)
        nc.vector.transpose(row_number[:], column_number[:])
        for g in range(GROUPS):
            block = slice(g * GROUP, (g + 1) * GROUP)
            nc.vector.tensor_tensor(identity[block, block], row_number[block, :], column_number[block, :], IS_EQUAL)
        primed = held.tile([D, 1], F32, name="primed")
        nc.scalar.activation(primed[:], zeros[:], IDENTITY)
        unread = layer1.tile([D, S], F32, name="unread", tag="pre")
        for turn in range(WARM):
            for g in range(GROUPS):
                nc.tensor.matmul(
                    unread[g * GROUP : (g + 1) * GROUP, :],
                    zeros[:].to_broadcast([D, GROUP]),
                    zeros[:].to_broadcast([D, S]),
                    start=True,
                    stop=True,
                )

        pre = []
        ctx_rows = spread.tile([D, D], F32, name="ctx_rows")
        for i in range(PIECES):
            pre.append(layer1.tile([D, PIECE], F32, name="pre"))
            entries = offsets[:, i * (PIECE // 16) : (i + 1) * (PIECE // 16)]
            nc.tensor.matmul(pre[i][:], wq_sb[:], table_sb[:].indirect(entries), start=True, stop=False)
            if i == 0:
                nc.tensor.transpose(ctx_rows[:], ctx_sb[:].to_broadcast([D, D]), identity[:])

        products = held.tile([D, D], F32, name="products")
        v_sb = held.tile([D, 1], F32, name="v_sb")
        nc.vector.scalar_tensor_tensor(products[:], w2_sb[:], 1.0, ctx_rows[:], MULT, MULT, accum_out=v_sb[:])
        v_high = held.tile([D, 1], BF16, name="v_high")
        v_low = held.tile([D, 1], BF16, name="v_low")
        nc.vector.tensor_copy(v_high[:], v_sb[:])
        nc.vector.tensor_tensor(v_low[:], v_sb[:], v_high[:], SUBTRACT)

        def bias_relu(i, h_i, pre_i):
            if i % 2 == 0:
                nc.vector.tensor_scalar(h_i, pre_i, b1_sb[:], 0.0, ADD, MAX)
            else:
                nc.scalar.activation(h_i, pre_i, RELU, bias=b1_sb[:])

        def add_c(i, logits_i, sums_i):
            if i % 2 == 0:
                nc.vector.tensor_scalar_add(logits_i, sums_i, c_sb[:])
            else:
                nc.scalar.activation(logits_i, sums_i, IDENTITY, bias=c_sb[:])

        h = []
        for i in range(PIECES):
            nc.tensor.matmul(pre[i][:], wp_sb[:], qpu_sb[:, i * PIECE : (i + 1) * PIECE], start=False, stop=True)
            h.append(work.tile([D, PIECE], BF16, name="h"))
            bias_relu(i, h[i][:], pre[i][:])

        c_sb = held.tile([D, 1], F32, name="c_sb")
        nc.vector.scalar_tensor_tensor(products[:], b2_firsts[:], 1.0, ctx_rows[:], MULT, MULT, accum_out=c_sb[:])
        for pair in range(N // PAIR):
            sums = summed.tile([D, SHARE], F32, name="sums")
            for step, part in enumerate((v_high, v_low)):
                for g in range(GROUPS):
                    i, half = 2 * pair + g // 2, g % 2
                    nc.tensor.matmul(
                        sums[g * GROUP : (g + 1) * GROUP, :],
                        part[:].to_broadcast([D, GROUP]),
                        h[i][:, half * SHARE : (half + 1) * SHARE],
                        start=step == 0,
                        stop=step == 1,
                    )
            logits = work.tile([D, SHARE], F32, name="logits")
            add_c(pair, logits[:], sums[:])
            queue = nc.sync if pair % 2 == 0 else nc.scalar
            queue.dma_start(
                out[:, pair * PAIR : (pair + 1) * PAIR].rearrange("o (g x) -> (o g) x", g=GROUPS),
                logits[0:D:GROUP, :],
            )
